import numpy as np
import ml_dtypes


def mxq(x, axis, fmt="e4m3"):
    dtype, down = {"e4m3": (ml_dtypes.float8_e4m3fn, 7), "e5m2": (ml_dtypes.float8_e5m2, 14)}[fmt]
    v = np.moveaxis(np.asarray(x, np.float32).astype(ml_dtypes.bfloat16).astype(np.float64), axis, -1)
    blocks = v.reshape(v.shape[:-1] + (-1, 32))
    amax = np.abs(blocks).max(-1, keepdims=True)
    byte = np.maximum(np.where(amax > 0, np.frexp(amax)[1] - 1 + 127, 0) - down, 1)
    scale = np.exp2(byte - 127.0)
    codes = (blocks / scale).astype(np.float32).astype(dtype).astype(np.float64)
    return np.moveaxis((codes * scale).reshape(v.shape), -1, axis)


WIDE = False


def mx_kscale(k):
    if not WIDE:
        return np.ones(k)
    levels = np.array([10, -10, 5, -5, 0])
    a = np.random.permutation(np.resize(levels, k // 512 * 4)).reshape(k // 512, 4)
    idx = np.arange(k)
    return np.exp2(a[idx // 512, idx % 128 // 32])


BF16 = ml_dtypes.bfloat16


def bf(x):
    return np.asarray(x, np.float32).astype(BF16)


def f64(x):
    return np.asarray(x).astype(np.float64)


D, KW, STRIDE, STACK, B, O = 32, 11, 3, 8, 4096, 128
W_IN = D * D
POS = (D - KW) // STRIDE + 1
K = STACK * POS * POS


def build_mask():
    base_new = np.tile(np.arange(KW), KW)
    addition_new = np.repeat(np.arange(KW) * D, KW)
    index_1 = addition_new + base_new
    index_width = np.tile(index_1, POS)
    addition_width = np.repeat(STRIDE * np.arange(POS), KW * KW)
    index_row = index_width + addition_width
    index_column = np.tile(index_row, POS)
    addition_height = np.repeat(STRIDE * D * np.arange(POS), KW * KW * POS)
    index_final = index_column + addition_height
    stack = np.repeat(np.arange(POS * POS), KW * KW)
    block = np.zeros((POS * POS, W_IN))
    block[stack, index_final] = 1.0
    return np.vstack([block] * STACK)


def setup_inputs():
    s = mx_kscale(W_IN)
    return {"z": bf(np.random.standard_normal((B, W_IN)) * s),
            "T1": bf(np.random.standard_normal((K, W_IN)) * 0.7 / np.sqrt(KW * KW) / s),
            "T2": bf(np.random.standard_normal((K, W_IN)) * 0.7 / np.sqrt(KW * KW) / s),
            "T0": bf(np.random.standard_normal(K)),
            "mask": bf(build_mask())}


def reference(z, T1, T2, T0, mask):
    zq = mxq(f64(z).reshape(-1, D * D), 1, "e4m3")
    m = f64(mask)
    x1 = zq @ mxq(m * f64(T1), 1, "e4m3").T
    x2 = 2.0 * (zq @ mxq(m * f64(T2), 1, "e4m3").T) * x1 - f64(T0)
    return x1, x2

@@ -1,0 +1,209 @@
+from contextlib import ExitStack
+
+import concourse.mybir as mybir
+from concourse.masks import make_identity
+
+F32 = mybir.dt.float32
+BF16 = mybir.dt.bfloat16
+U32 = mybir.dt.uint32
+U8 = mybir.dt.uint8
+FP8X4 = mybir.dt.float8_e4m3fn_x4
+ALU = mybir.AluOpType
+
+P = 128
+B, K, O = 4096, 1024, 512
+NT = B // P
+NB = 2
+STACKS, PAIRS, Q = 8, 4, 16
+WIN = 448
+WSTEP = 192
+PAIR_G = ((0,), (0, 1), (0, 1), (1,))
+ZCHUNKS = (2, 2, 4, 4, 4, 4, 4, 4, 4)
+
+FLOPS = 2 * 2 * B * K * O
+BYTES = B * K * 2 + 3 * O * 352 * 2 + O * 2 + 2 * B * O * 4
+
+
+def unit(w, g, i):
+    if i == 0:
+        return w
+    if i == 3:
+        return 10 + w
+    return 2 + 4 * w + 2 * g + (i - 1)
+
+
+def tile_chebyshev_l3_sparsed32_stack_pa_t_kernel(tc, z, T1, T2, T0, mask, out_0, out_1):
+    nc = tc.nc
+    with ExitStack() as ctx:
+        const = ctx.enter_context(tc.tile_pool(name="const", bufs=1))
+        wpool = ctx.enter_context(tc.tile_pool(name="wpool", bufs=1))
+        zpool = ctx.enter_context(tc.tile_pool(name="zpool", bufs=1))
+        gpool = ctx.enter_context(tc.tile_pool(name="gpool", bufs=3))
+        opool = ctx.enter_context(tc.tile_pool(name="opool", bufs=6))
+        ps_t = ctx.enter_context(tc.psum_pool(name="ps_t", bufs=2))
+        ps_a = ctx.enter_context(tc.psum_pool(name="ps_a", bufs=3))
+
+        views = [a.rearrange("(s i q) k -> i q s k", s=STACKS, i=PAIRS, q=Q) for a in (mask, T1, T2)]
+        raw = []
+        for i in range(PAIRS):
+            r = wpool.tile([P, 3, WIN], BF16, name="raw%d" % i)
+            raw.append(r)
+            for a in range(3):
+                nc.sync.dma_start(out=r[:, a, :], in_=views[a][i, :, :, WSTEP * i : WSTEP * i + WIN])
+        zv = z.rearrange("(p j) k -> p j k", j=NT)
+        where = []
+        j0 = 0
+        for n, nj in enumerate(ZCHUNKS):
+            zt_sb = zpool.tile([P, nj, K], BF16, name="z%d" % n)
+            nc.sync.dma_start(out=zt_sb[:], in_=zv[:, j0 : j0 + nj, :])
+            for s in range(nj):
+                where.append((zt_sb, s))
+            j0 += nj
+
+        warm = const.tile([P, 8], F32, name="warm")
+        warm2 = const.tile([P, 8], F32, name="warm2")
+        nc.vector.memset(warm[:], 0.0)
+        nc.scalar.copy(out=warm2[:], in_=warm[:])
+        ident = const.tile([P, P], F32, name="ident")
+        make_identity(nc, ident[:])
+        t0row = const.tile([P, O], BF16, name="t0row")
+        nc.vector.memset(t0row[:], 0.0)
+        nc.scalar.dma_start(out=t0row[0:1, :], in_=T0.rearrange("(a n) -> a n", a=1))
+        ones = const.tile([P, P], BF16, name="ones")
+        nc.vector.memset(ones[:], 1.0)
+        prod = []
+        for i in range(PAIRS):
+            pr = wpool.tile([P, 2, 512 * len(PAIR_G[i])], BF16, name="prod%d" % i)
+            nc.vector.memset(pr[:], 0.0)
+            prod.append(pr)
+
+        wg = wpool.tile([P, 12, 512], BF16, name="wg", align_bytes=64)
+        wgw = wg[:].bitcast(F32)
+        wc = wpool.tile([P, 12 * P], U32, name="wc", align_bytes=64)
+        ws = wpool.tile([P, 12 * P], U8, name="ws", align_bytes=64)
+
+        def quantise_units(u0, nu):
+            nc.vector.quantize_mx(
+                out=wc[:, u0 * P : (u0 + nu) * P].bitcast(FP8X4),
+                scales=ws[:, u0 * P : (u0 + nu) * P],
+                in_=wg[:, u0 : u0 + nu, :].rearrange("p a b -> p (a b)"),
+            )
+
+        bank = 0
+        for i in range(PAIRS):
+            kbase = 512 * PAIR_G[i][0]
+            off = WSTEP * i - kbase
+            nc.vector.tensor_tensor(
+                out=prod[i][:, :, off : off + WIN],
+                in0=raw[i][:, 1:3, :],
+                in1=raw[i][:, 0:1, :].to_broadcast([P, 2, WIN]),
+                op=ALU.mult,
+            )
+            for g in PAIR_G[i]:
+                wt = ps_a.tile([P, 4, P], F32, name="wt", tag=("x1", "y2")[bank % 2])
+                bank += 1
+                for w in range(2):
+                    words = prod[i][:, w, :].bitcast(F32)
+                    for u in range(2):
+                        c0 = (512 * g + 256 * u - kbase) // 2
+                        nc.tensor.transpose(wt[:, 2 * w + u, :], words[:, c0 : c0 + P], ident[:])
+                for w in range(2):
+                    dst = wgw[:, unit(w, g, i), :].rearrange("p (s q u) -> p s q u", s=STACKS, q=Q, u=2)
+                    src = wt[:, 2 * w : 2 * w + 2, :].rearrange("p u (q s) -> p s q u", q=Q, s=STACKS)
+                    if w == 0:
+                        nc.scalar.copy(out=dst, in_=src)
+                    else:
+                        nc.vector.tensor_copy(out=dst, in_=src)
+            if i == 0 or i == 3:
+                quantise_units(unit(0, PAIR_G[i][0], i), 2)
+            else:
+                for w in range(2):
+                    for g in range(2):
+                        quantise_units(unit(w, g, i), 1)
+
+        t0ps = ps_t.tile([P, O], F32, name="t0ps", tag="zt")
+        nc.tensor.matmul(out=t0ps[:], lhsT=ones[:], rhs=t0row[:], start=True, stop=True)
+        t0b = const.tile([P, O], F32, name="t0b")
+        nc.scalar.copy(out=t0b[:], in_=t0ps[:])
+
+        o0v = out_0.rearrange("(p j) o -> p j o", j=NT)
+        o1v = out_1.rearrange("(p j) o -> p j o", j=NT)
+
+        def front(n):
+            zg = gpool.tile([P, NB, K], BF16, name="zg", align_bytes=64)
+            zgw = zg[:].bitcast(F32)
+            zts = []
+            for jj in range(NB):
+                src, slot = where[NB * n + jj]
+                words = src[:, slot, :].bitcast(F32)
+                zt = ps_t.tile([P, 4, P], F32, name="zt")
+                zts.append(zt)
+                for c in range(4):
+                    nc.tensor.transpose(zt[:, c, :], words[:, P * c : P * (c + 1)], ident[:])
+            for jj in range(NB):
+                nc.scalar.copy(
+                    out=zgw[:, jj, :].rearrange("p (g b u) -> p g b u", g=2, b=P, u=2),
+                    in_=zts[jj][:].rearrange("p (g u) b -> p g b u", g=2, u=2),
+                )
+            zc = gpool.tile([P, NB * 2 * P], U32, name="zc", align_bytes=64)
+            zs = gpool.tile([P, NB * 2 * P], U8, name="zs", align_bytes=64)
+            nc.vector.quantize_mx(
+                out=zc[:].bitcast(FP8X4), scales=zs[:], in_=zg[:].rearrange("p j k -> p (j k)")
+            )
+            return zc, zs
+
+        def back(n, zc, zs):
+            x1s = opool.tile([P, NB, O], F32, name="x1s")
+            x2s = opool.tile([P, NB, O], F32, name="x2s")
+            accs = []
+            for jj in range(NB):
+                x1 = ps_a.tile([P, O], F32, name="x1")
+                y2 = ps_a.tile([P, O], F32, name="y2")
+                accs.append((x1, y2))
+                for w in range(2):
+                    acc = accs[jj][w]
+                    for c0, c1, g, u0, start, stop in (
+                        (0, 128, 0, unit(w, 0, 0), True, True),
+                        (128, 384, 0, unit(w, 0, 1), True, False),
+                        (128, 384, 1, unit(w, 1, 1), False, True),
+                        (384, 512, 1, unit(w, 1, 3), True, True),
+                    ):
+                        l0 = (2 * jj + g) * P
+                        r0 = u0 * P
+                        nc.tensor.matmul_mx(
+                            out=acc[:, c0:c1],
+                            lhsT=zc[:, l0 : l0 + P].bitcast(FP8X4),
+                            lhsT_scale=zs[:, l0 : l0 + P],
+                            rhs=wc[:, r0 : r0 + c1 - c0].bitcast(FP8X4),
+                            rhs_scale=ws[:, r0 : r0 + c1 - c0],
+                            start=start,
+                            stop=stop,
+                        )
+            for jj in range(NB):
+                x1, y2 = accs[jj]
+                nat1 = x1s[:, jj, :].rearrange("p (s i q) -> p s i q", s=STACKS, i=PAIRS, q=Q)
+                nat2 = x2s[:, jj, :].rearrange("p (s i q) -> p s i q", s=STACKS, i=PAIRS, q=Q)
+                nc.scalar.copy(out=nat1, in_=x1[:].rearrange("p (i s q) -> p s i q", s=STACKS, i=PAIRS, q=Q))
+                nc.vector.tensor_tensor(
+                    out=nat2,
+                    in0=y2[:].rearrange("p (i s q) -> p s i q", s=STACKS, i=PAIRS, q=Q),
+                    in1=nat1,
+                    op=ALU.mult,
+                )
+            nc.sync.dma_start(out=o0v[:, NB * n : NB * (n + 1), :], in_=x1s[:])
+            nc.vector.scalar_tensor_tensor(
+                out=x2s[:],
+                in0=x2s[:],
+                scalar=2.0,
+                in1=t0b[:].unsqueeze(1).to_broadcast([P, NB, O]),
+                op0=ALU.mult,
+                op1=ALU.subtract,
+            )
+            nc.sync.dma_start(out=o1v[:, NB * n : NB * (n + 1), :], in_=x2s[:])
+
+        nbunch = NT // NB
+        cur = front(0)
+        for n in range(nbunch):
+            nxt = front(n + 1) if n + 1 < nbunch else None
+            back(n, cur[0], cur[1])
+            cur = nxt

@@ -39,7 +39,7 @@ def tile_chebyshev_l3_sparsed32_stack_pa_t_kernel(tc, z, T1, T2, T0, mask, out_0
         wpool = ctx.enter_context(tc.tile_pool(name="wpool", bufs=1))
         zpool = ctx.enter_context(tc.tile_pool(name="zpool", bufs=1))
         gpool = ctx.enter_context(tc.tile_pool(name="gpool", bufs=3))
-        opool = ctx.enter_context(tc.tile_pool(name="opool", bufs=6))
+        opool = ctx.enter_context(tc.tile_pool(name="opool", bufs=8))
         ps_t = ctx.enter_context(tc.psum_pool(name="ps_t", bufs=2))
         ps_a = ctx.enter_context(tc.psum_pool(name="ps_a", bufs=3))
 
@@ -67,14 +67,14 @@ def tile_chebyshev_l3_sparsed32_stack_pa_t_kernel(tc, z, T1, T2, T0, mask, out_0
         ident = const.tile([P, P], F32, name="ident")
         make_identity(nc, ident[:])
         t0row = const.tile([P, O], BF16, name="t0row")
-        nc.vector.memset(t0row[:], 0.0)
+        nc.vector.memset(t0row[:].bitcast(F32), 0.0)
         nc.scalar.dma_start(out=t0row[0:1, :], in_=T0.rearrange("(a n) -> a n", a=1))
         ones = const.tile([P, P], BF16, name="ones")
         nc.vector.memset(ones[:], 1.0)
         prod = []
         for i in range(PAIRS):
             pr = wpool.tile([P, 2, 512 * len(PAIR_G[i])], BF16, name="prod%d" % i)
-            nc.vector.memset(pr[:], 0.0)
+            nc.vector.memset(pr[:].bitcast(F32), 0.0)
             prod.append(pr)
 
         wg = wpool.tile([P, 12, 512], BF16, name="wg", align_bytes=64)
@@ -89,31 +89,32 @@ def tile_chebyshev_l3_sparsed32_stack_pa_t_kernel(tc, z, T1, T2, T0, mask, out_0
                 in_=wg[:, u0 : u0 + nu, :].rearrange("p a b -> p (a b)"),
             )
 
-        bank = 0
-        for i in range(PAIRS):
-            kbase = 512 * PAIR_G[i][0]
-            off = WSTEP * i - kbase
+        def mask_pair(i):
+            off = WSTEP * i - 512 * PAIR_G[i][0]
             nc.vector.tensor_tensor(
                 out=prod[i][:, :, off : off + WIN],
                 in0=raw[i][:, 1:3, :],
                 in1=raw[i][:, 0:1, :].to_broadcast([P, 2, WIN]),
                 op=ALU.mult,
             )
+
+        def flip_pair(i):
+            kbase = 512 * PAIR_G[i][0]
             for g in PAIR_G[i]:
-                wt = ps_a.tile([P, 4, P], F32, name="wt", tag=("x1", "y2")[bank % 2])
-                bank += 1
+                wt = ps_a.tile([P, 4, P], F32, name="wt", tag=("x1", "y2")[(i + g) % 2])
                 for w in range(2):
                     words = prod[i][:, w, :].bitcast(F32)
                     for u in range(2):
                         c0 = (512 * g + 256 * u - kbase) // 2
                         nc.tensor.transpose(wt[:, 2 * w + u, :], words[:, c0 : c0 + P], ident[:])
-                for w in range(2):
-                    dst = wgw[:, unit(w, g, i), :].rearrange("p (s q u) -> p s q u", s=STACKS, q=Q, u=2)
-                    src = wt[:, 2 * w : 2 * w + 2, :].rearrange("p u (q s) -> p s q u", q=Q, s=STACKS)
-                    if w == 0:
-                        nc.scalar.copy(out=dst, in_=src)
-                    else:
-                        nc.vector.tensor_copy(out=dst, in_=src)
+                u0 = unit(0, g, i)
+                du = unit(1, g, i) - u0
+                nc.scalar.copy(
+                    out=wgw[:, u0 : u0 + du + 1 : du, :].rearrange("p w (c u) -> p w c u", u=2),
+                    in_=wt[:].rearrange("p (w u) c -> p w c u", u=2),
+                )
+
+        def quantise_pair(i):
             if i == 0 or i == 3:
                 quantise_units(unit(0, PAIR_G[i][0], i), 2)
             else:
@@ -121,15 +122,10 @@ def tile_chebyshev_l3_sparsed32_stack_pa_t_kernel(tc, z, T1, T2, T0, mask, out_0
                     for g in range(2):
                         quantise_units(unit(w, g, i), 1)
 
-        t0ps = ps_t.tile([P, O], F32, name="t0ps", tag="zt")
-        nc.tensor.matmul(out=t0ps[:], lhsT=ones[:], rhs=t0row[:], start=True, stop=True)
-        t0b = const.tile([P, O], F32, name="t0b")
-        nc.scalar.copy(out=t0b[:], in_=t0ps[:])
-
         o0v = out_0.rearrange("(p j) o -> p j o", j=NT)
         o1v = out_1.rearrange("(p j) o -> p j o", j=NT)
 
-        def front(n):
+        def front_flip(n):
             zg = gpool.tile([P, NB, K], BF16, name="zg", align_bytes=64)
             zgw = zg[:].bitcast(F32)
             zts = []
@@ -145,6 +141,9 @@ def tile_chebyshev_l3_sparsed32_stack_pa_t_kernel(tc, z, T1, T2, T0, mask, out_0
                     out=zgw[:, jj, :].rearrange("p (g b u) -> p g b u", g=2, b=P, u=2),
                     in_=zts[jj][:].rearrange("p (g u) b -> p g b u", g=2, u=2),
                 )
+            return zg
+
+        def front_quantise(zg):
             zc = gpool.tile([P, NB * 2 * P], U32, name="zc", align_bytes=64)
             zs = gpool.tile([P, NB * 2 * P], U8, name="zs", align_bytes=64)
             nc.vector.quantize_mx(
@@ -152,9 +151,7 @@ def tile_chebyshev_l3_sparsed32_stack_pa_t_kernel(tc, z, T1, T2, T0, mask, out_0
             )
             return zc, zs
 
-        def back(n, zc, zs):
-            x1s = opool.tile([P, NB, O], F32, name="x1s")
-            x2s = opool.tile([P, NB, O], F32, name="x2s")
+        def passes(zc, zs):
             accs = []
             for jj in range(NB):
                 x1 = ps_a.tile([P, O], F32, name="x1")
@@ -179,31 +176,63 @@ def tile_chebyshev_l3_sparsed32_stack_pa_t_kernel(tc, z, T1, T2, T0, mask, out_0
                             start=start,
                             stop=stop,
                         )
+            return accs
+
+        def products(n, accs):
+            x1s = opool.tile([P, NB, O], F32, name="x1s")
+            x2s = opool.tile([P, NB, O], F32, name="x2s")
             for jj in range(NB):
                 x1, y2 = accs[jj]
-                nat1 = x1s[:, jj, :].rearrange("p (s i q) -> p s i q", s=STACKS, i=PAIRS, q=Q)
-                nat2 = x2s[:, jj, :].rearrange("p (s i q) -> p s i q", s=STACKS, i=PAIRS, q=Q)
-                nc.scalar.copy(out=nat1, in_=x1[:].rearrange("p (i s q) -> p s i q", s=STACKS, i=PAIRS, q=Q))
-                nc.vector.tensor_tensor(
+                nat1 = x1s[:, jj, :].rearrange("p (s r) -> p s r", s=STACKS)
+                nat2 = x2s[:, jj, :].rearrange("p (s r) -> p s r", s=STACKS)
+                nc.scalar.copy(out=nat1, in_=x1[:].rearrange("p (r s) -> p s r", s=STACKS))
+                nc.vector.scalar_tensor_tensor(
                     out=nat2,
-                    in0=y2[:].rearrange("p (i s q) -> p s i q", s=STACKS, i=PAIRS, q=Q),
+                    in0=y2[:].rearrange("p (r s) -> p s r", s=STACKS),
+                    scalar=2.0,
                     in1=nat1,
-                    op=ALU.mult,
+                    op0=ALU.mult,
+                    op1=ALU.mult,
                 )
             nc.sync.dma_start(out=o0v[:, NB * n : NB * (n + 1), :], in_=x1s[:])
-            nc.vector.scalar_tensor_tensor(
-                out=x2s[:],
-                in0=x2s[:],
-                scalar=2.0,
-                in1=t0b[:].unsqueeze(1).to_broadcast([P, NB, O]),
-                op0=ALU.mult,
-                op1=ALU.subtract,
-            )
+            return x2s
+
+        def finish(n, x2s):
+            for jj in range(NB):
+                eng = nc.gpsimd if (NB * n + jj) % 2 == 1 else nc.vector
+                for h in range(1):
+                    cols = slice(h * (O // 1), (h + 1) * (O // 1))
+                    eng.tensor_tensor(out=x2s[:, jj, cols], in0=x2s[:, jj, cols], in1=t0b[:, cols], op=ALU.subtract)
             nc.sync.dma_start(out=o1v[:, NB * n : NB * (n + 1), :], in_=x2s[:])
 
+        mask_pair(0)
+        flip_pair(0)
+        mask_pair(1)
+        flip_pair(1)
+        quantise_pair(0)
+        mask_pair(2)
+        flip_pair(2)
+        quantise_pair(1)
+        mask_pair(3)
+        flip_pair(3)
+        quantise_pair(2)
+        zg0 = front_flip(0)
+        quantise_pair(3)
+        cur = front_quantise(zg0)
+
+        t0ps = ps_t.tile([P, O], F32, name="t0ps", tag="zt")
+        nc.tensor.matmul(out=t0ps[:], lhsT=ones[:], rhs=t0row[:], start=True, stop=True)
+        t0b = const.tile([P, O], F32, name="t0b")
+        nc.scalar.copy(out=t0b[:], in_=t0ps[:])
+
         nbunch = NT // NB
-        cur = front(0)
+        late = None
         for n in range(nbunch):
-            nxt = front(n + 1) if n + 1 < nbunch else None
-            back(n, cur[0], cur[1])
-            cur = nxt
+            zg = front_flip(n + 1) if n + 1 < nbunch else None
+            accs = passes(cur[0], cur[1])
+            if zg is not None:
+                cur = front_quantise(zg)
+            if late is not None:
+                finish(n - 1, late)
+            late = products(n, accs)
+        finish(nbunch - 1, late)

@@ -18,7 +18,8 @@ STACKS, PAIRS, Q = 8, 4, 16
 WIN = 448
 WSTEP = 192
 PAIR_G = ((0,), (0, 1), (0, 1), (1,))
-ZCHUNKS = (2, 2, 4, 4, 4, 4, 4, 4, 4)
+ZCHUNKS = (2, 2, 4, 8, 8, 8)
+GROUPS = (2, 2, 2, 2, 2, 2, 2, 1, 1)
 
 FLOPS = 2 * 2 * B * K * O
 BYTES = B * K * 2 + 3 * O * 352 * 2 + O * 2 + 2 * B * O * 4
@@ -39,9 +40,12 @@ def tile_chebyshev_l3_sparsed32_stack_pa_t_kernel(tc, z, T1, T2, T0, mask, out_0
         wpool = ctx.enter_context(tc.tile_pool(name="wpool", bufs=1))
         zpool = ctx.enter_context(tc.tile_pool(name="zpool", bufs=1))
         gpool = ctx.enter_context(tc.tile_pool(name="gpool", bufs=3))
-        opool = ctx.enter_context(tc.tile_pool(name="opool", bufs=8))
+        opool = ctx.enter_context(tc.tile_pool(name="opool", bufs=5))
         ps_t = ctx.enter_context(tc.psum_pool(name="ps_t", bufs=2))
-        ps_a = ctx.enter_context(tc.psum_pool(name="ps_a", bufs=3))
+        ps_x = ctx.enter_context(tc.psum_pool(name="ps_x", bufs=2))
+        ps_y = ctx.enter_context(tc.psum_pool(name="ps_y", bufs=3))
+        ps_c = ctx.enter_context(tc.psum_pool(name="ps_c", bufs=1))
+        ctx.enter_context(tc.manual_schedule())
 
         views = [a.rearrange("(s i q) k -> i q s k", s=STACKS, i=PAIRS, q=Q) for a in (mask, T1, T2)]
         raw = []
@@ -101,7 +105,10 @@ def tile_chebyshev_l3_sparsed32_stack_pa_t_kernel(tc, z, T1, T2, T0, mask, out_0
         def flip_pair(i):
             kbase = 512 * PAIR_G[i][0]
             for g in PAIR_G[i]:
-                wt = ps_a.tile([P, 4, P], F32, name="wt", tag=("x1", "y2")[(i + g) % 2])
+                if (i + g) % 2 == 0:
+                    wt = ps_y.tile([P, 4, P], F32, name="wt", tag="y2")
+                else:
+                    wt = ps_x.tile([P, 4, P], F32, name="wt", tag="x1")
                 for w in range(2):
                     words = prod[i][:, w, :].bitcast(F32)
                     for u in range(2):
@@ -154,8 +161,8 @@ def tile_chebyshev_l3_sparsed32_stack_pa_t_kernel(tc, z, T1, T2, T0, mask, out_0
         def passes(zc, zs):
             accs = []
             for jj in range(NB):
-                x1 = ps_a.tile([P, O], F32, name="x1")
-                y2 = ps_a.tile([P, O], F32, name="y2")
+                x1 = ps_x.tile([P, O], F32, name="x1")
+                y2 = ps_y.tile([P, O], F32, name="y2")
                 accs.append((x1, y2))
                 for w in range(2):
                     acc = accs[jj][w]
@@ -178,13 +185,26 @@ def tile_chebyshev_l3_sparsed32_stack_pa_t_kernel(tc, z, T1, T2, T0, mask, out_0
                         )
             return accs
 
+        nbunch = NT // NB
+        span = []
+        for size in GROUPS:
+            first = len(span)
+            for k in range(size):
+                span.append((first, size))
+        outs = {}
+
         def products(n, accs):
-            x1s = opool.tile([P, NB, O], F32, name="x1s")
-            x2s = opool.tile([P, NB, O], F32, name="x2s")
+            first, size = span[n]
+            if n == first:
+                x1new = opool.tile([P, size * NB, O], F32, name="x1s")
+                x2new = opool.tile([P, size * NB, O], F32, name="x2s")
+                outs[first] = (x1new, x2new)
+            x1s, x2s = outs[first]
             for jj in range(NB):
                 x1, y2 = accs[jj]
-                nat1 = x1s[:, jj, :].rearrange("p (s r) -> p s r", s=STACKS)
-                nat2 = x2s[:, jj, :].rearrange("p (s r) -> p s r", s=STACKS)
+                slot = (n - first) * NB + jj
+                nat1 = x1s[:, slot, :].rearrange("p (s r) -> p s r", s=STACKS)
+                nat2 = x2s[:, slot, :].rearrange("p (s r) -> p s r", s=STACKS)
                 nc.scalar.copy(out=nat1, in_=x1[:].rearrange("p (r s) -> p s r", s=STACKS))
                 nc.vector.scalar_tensor_tensor(
                     out=nat2,
@@ -194,16 +214,26 @@ def tile_chebyshev_l3_sparsed32_stack_pa_t_kernel(tc, z, T1, T2, T0, mask, out_0
                     op0=ALU.mult,
                     op1=ALU.mult,
                 )
-            nc.sync.dma_start(out=o0v[:, NB * n : NB * (n + 1), :], in_=x1s[:])
-            return x2s
+            if n == first + size - 1:
+                nc.sync.dma_start(out=o0v[:, NB * first : NB * (first + size), :], in_=x1s[:])
 
-        def finish(n, x2s):
+        def finish(n):
+            first, size = span[n]
+            x2s = outs[first][1]
             for jj in range(NB):
-                eng = nc.gpsimd if (NB * n + jj) % 2 == 1 else nc.vector
-                for h in range(1):
-                    cols = slice(h * (O // 1), (h + 1) * (O // 1))
-                    eng.tensor_tensor(out=x2s[:, jj, cols], in0=x2s[:, jj, cols], in1=t0b[:, cols], op=ALU.subtract)
-            nc.sync.dma_start(out=o1v[:, NB * n : NB * (n + 1), :], in_=x2s[:])
+                slot = (n - first) * NB + jj
+                if jj == 1 and n < nbunch - 1:
+                    for h in range(2):
+                        cols = slice(h * (O // 2), (h + 1) * (O // 2))
+                        nc.gpsimd.tensor_tensor(
+                            out=x2s[:, slot, cols], in0=x2s[:, slot, cols], in1=t0b[:, cols], op=ALU.subtract
+                        )
+                else:
+                    nc.vector.tensor_tensor(
+                        out=x2s[:, slot, :], in0=x2s[:, slot, :], in1=t0ps[:], op=ALU.subtract
+                    )
+            if n == first + size - 1:
+                nc.sync.dma_start(out=o1v[:, NB * first : NB * (first + size), :], in_=x2s[:])
 
         mask_pair(0)
         flip_pair(0)
@@ -220,19 +250,17 @@ def tile_chebyshev_l3_sparsed32_stack_pa_t_kernel(tc, z, T1, T2, T0, mask, out_0
         quantise_pair(3)
         cur = front_quantise(zg0)
 
-        t0ps = ps_t.tile([P, O], F32, name="t0ps", tag="zt")
+        t0ps = ps_c.tile([P, O], F32, name="t0ps")
         nc.tensor.matmul(out=t0ps[:], lhsT=ones[:], rhs=t0row[:], start=True, stop=True)
         t0b = const.tile([P, O], F32, name="t0b")
         nc.scalar.copy(out=t0b[:], in_=t0ps[:])
 
-        nbunch = NT // NB
-        late = None
         for n in range(nbunch):
             zg = front_flip(n + 1) if n + 1 < nbunch else None
             accs = passes(cur[0], cur[1])
             if zg is not None:
                 cur = front_quantise(zg)
-            if late is not None:
-                finish(n - 1, late)
-            late = products(n, accs)
-        finish(nbunch - 1, late)
+            if n > 0:
+                finish(n - 1)
+            products(n, accs)
+        finish(nbunch - 1)

@@ -13,13 +13,13 @@ ALU = mybir.AluOpType
 P = 128
 B, K, O = 4096, 1024, 512
 NT = B // P
-NB = 2
 STACKS, PAIRS, Q = 8, 4, 16
 WIN = 448
 WSTEP = 192
 PAIR_G = ((0,), (0, 1), (0, 1), (1,))
-ZCHUNKS = (2, 2, 4, 8, 8, 8)
-GROUPS = (2, 2, 2, 2, 2, 2, 2, 1, 1)
+BUNCHES = (1, 2, 2, 2, 2, 2, 2, 2, 2, 2, 2, 2, 2, 2, 2, 2, 1)
+ZCHUNKS = (1, 2, 4, 8, 8, 9)
+GROUPS = (4, 4, 4, 4, 4, 4, 4, 2, 1, 1)
 
 FLOPS = 2 * 2 * B * K * O
 BYTES = B * K * 2 + 3 * O * 352 * 2 + O * 2 + 2 * B * O * 4
@@ -56,13 +56,12 @@ def tile_chebyshev_l3_sparsed32_stack_pa_t_kernel(tc, z, T1, T2, T0, mask, out_0
                 nc.sync.dma_start(out=r[:, a, :], in_=views[a][i, :, :, WSTEP * i : WSTEP * i + WIN])
         zv = z.rearrange("(p j) k -> p j k", j=NT)
         where = []
-        j0 = 0
         for n, nj in enumerate(ZCHUNKS):
+            j0 = len(where)
             zt_sb = zpool.tile([P, nj, K], BF16, name="z%d" % n)
             nc.sync.dma_start(out=zt_sb[:], in_=zv[:, j0 : j0 + nj, :])
             for s in range(nj):
                 where.append((zt_sb, s))
-            j0 += nj
 
         warm = const.tile([P, 8], F32, name="warm")
         warm2 = const.tile([P, 8], F32, name="warm2")
@@ -129,38 +128,43 @@ def tile_chebyshev_l3_sparsed32_stack_pa_t_kernel(tc, z, T1, T2, T0, mask, out_0
                     for g in range(2):
                         quantise_units(unit(w, g, i), 1)
 
-        o0v = out_0.rearrange("(p j) o -> p j o", j=NT)
-        o1v = out_1.rearrange("(p j) o -> p j o", j=NT)
+        tiles_of = []
+        for size in BUNCHES:
+            j0 = sum(len(t) for t in tiles_of)
+            tiles_of.append(list(range(j0, j0 + size)))
+        nbunch = len(tiles_of)
 
         def front_flip(n):
-            zg = gpool.tile([P, NB, K], BF16, name="zg", align_bytes=64)
+            tiles = tiles_of[n]
+            zg = gpool.tile([P, len(tiles), K], BF16, name="zg", align_bytes=64)
             zgw = zg[:].bitcast(F32)
             zts = []
-            for jj in range(NB):
-                src, slot = where[NB * n + jj]
+            for j in tiles:
+                src, slot = where[j]
                 words = src[:, slot, :].bitcast(F32)
                 zt = ps_t.tile([P, 4, P], F32, name="zt")
                 zts.append(zt)
                 for c in range(4):
                     nc.tensor.transpose(zt[:, c, :], words[:, P * c : P * (c + 1)], ident[:])
-            for jj in range(NB):
+            for jj in range(len(tiles)):
                 nc.scalar.copy(
                     out=zgw[:, jj, :].rearrange("p (g b u) -> p g b u", g=2, b=P, u=2),
                     in_=zts[jj][:].rearrange("p (g u) b -> p g b u", g=2, u=2),
                 )
             return zg
 
-        def front_quantise(zg):
-            zc = gpool.tile([P, NB * 2 * P], U32, name="zc", align_bytes=64)
-            zs = gpool.tile([P, NB * 2 * P], U8, name="zs", align_bytes=64)
+        def front_quantise(n, zg):
+            width = len(tiles_of[n]) * 2 * P
+            zc = gpool.tile([P, width], U32, name="zc", align_bytes=64)
+            zs = gpool.tile([P, width], U8, name="zs", align_bytes=64)
             nc.vector.quantize_mx(
                 out=zc[:].bitcast(FP8X4), scales=zs[:], in_=zg[:].rearrange("p j k -> p (j k)")
             )
             return zc, zs
 
-        def passes(zc, zs):
+        def passes(n, zc, zs):
             accs = []
-            for jj in range(NB):
+            for jj in range(len(tiles_of[n])):
                 x1 = ps_x.tile([P, O], F32, name="x1")
                 y2 = ps_y.tile([P, O], F32, name="y2")
                 accs.append((x1, y2))
@@ -185,55 +189,49 @@ def tile_chebyshev_l3_sparsed32_stack_pa_t_kernel(tc, z, T1, T2, T0, mask, out_0
                         )
             return accs
 
-        nbunch = NT // NB
+        o0v = out_0.rearrange("(p j) o -> p j o", j=NT)
+        o1v = out_1.rearrange("(p j) o -> p j o", j=NT)
         span = []
         for size in GROUPS:
             first = len(span)
             for k in range(size):
                 span.append((first, size))
         outs = {}
+        left = {}
 
-        def products(n, accs):
-            first, size = span[n]
-            if n == first:
-                x1new = opool.tile([P, size * NB, O], F32, name="x1s")
-                x2new = opool.tile([P, size * NB, O], F32, name="x2s")
+        def product(j, acc):
+            first, size = span[j]
+            if j == first:
+                x1new = opool.tile([P, size, O], F32, name="x1s")
+                x2new = opool.tile([P, size, O], F32, name="x2s")
                 outs[first] = (x1new, x2new)
+                left[first] = size
             x1s, x2s = outs[first]
-            for jj in range(NB):
-                x1, y2 = accs[jj]
-                slot = (n - first) * NB + jj
-                nat1 = x1s[:, slot, :].rearrange("p (s r) -> p s r", s=STACKS)
-                nat2 = x2s[:, slot, :].rearrange("p (s r) -> p s r", s=STACKS)
-                nc.scalar.copy(out=nat1, in_=x1[:].rearrange("p (r s) -> p s r", s=STACKS))
-                nc.vector.scalar_tensor_tensor(
-                    out=nat2,
-                    in0=y2[:].rearrange("p (r s) -> p s r", s=STACKS),
-                    scalar=2.0,
-                    in1=nat1,
-                    op0=ALU.mult,
-                    op1=ALU.mult,
-                )
-            if n == first + size - 1:
-                nc.sync.dma_start(out=o0v[:, NB * first : NB * (first + size), :], in_=x1s[:])
+            nat1 = x1s[:, j - first, :].rearrange("p (s r) -> p s r", s=STACKS)
+            nat2 = x2s[:, j - first, :].rearrange("p (s r) -> p s r", s=STACKS)
+            nc.scalar.copy(out=nat1, in_=acc[0][:].rearrange("p (r s) -> p s r", s=STACKS))
+            nc.vector.scalar_tensor_tensor(
+                out=nat2,
+                in0=acc[1][:].rearrange("p (r s) -> p s r", s=STACKS),
+                scalar=2.0,
+                in1=nat1,
+                op0=ALU.mult,
+                op1=ALU.mult,
+            )
+            if j == first + size - 1:
+                nc.sync.dma_start(out=o0v[:, first : first + size, :], in_=x1s[:])
 
-        def finish(n):
-            first, size = span[n]
+        def subtract(j, on_gpsimd):
+            first, size = span[j]
             x2s = outs[first][1]
-            for jj in range(NB):
-                slot = (n - first) * NB + jj
-                if jj == 1 and n < nbunch - 1:
-                    for h in range(2):
-                        cols = slice(h * (O // 2), (h + 1) * (O // 2))
-                        nc.gpsimd.tensor_tensor(
-                            out=x2s[:, slot, cols], in0=x2s[:, slot, cols], in1=t0b[:, cols], op=ALU.subtract
-                        )
-                else:
-                    nc.vector.tensor_tensor(
-                        out=x2s[:, slot, :], in0=x2s[:, slot, :], in1=t0ps[:], op=ALU.subtract
-                    )
-            if n == first + size - 1:
-                nc.sync.dma_start(out=o1v[:, NB * first : NB * (first + size), :], in_=x2s[:])
+            row = x2s[:, j - first, :]
+            if on_gpsimd:
+                nc.gpsimd.tensor_tensor(out=row, in0=row, in1=t0b[:], op=ALU.subtract)
+            else:
+                nc.vector.tensor_tensor(out=row, in0=row, in1=t0ps[:], op=ALU.subtract)
+            left[first] = left[first] - 1
+            if left[first] == 0:
+                nc.sync.dma_start(out=o1v[:, first : first + size, :], in_=x2s[:])
 
         mask_pair(0)
         flip_pair(0)
@@ -248,19 +246,25 @@ def tile_chebyshev_l3_sparsed32_stack_pa_t_kernel(tc, z, T1, T2, T0, mask, out_0
         quantise_pair(2)
         zg0 = front_flip(0)
         quantise_pair(3)
-        cur = front_quantise(zg0)
+        cur = front_quantise(0, zg0)
 
         t0ps = ps_c.tile([P, O], F32, name="t0ps")
         nc.tensor.matmul(out=t0ps[:], lhsT=ones[:], rhs=t0row[:], start=True, stop=True)
         t0b = const.tile([P, O], F32, name="t0b")
         nc.scalar.copy(out=t0b[:], in_=t0ps[:])
 
+        owed = []
         for n in range(nbunch):
+            tiles = tiles_of[n]
             zg = front_flip(n + 1) if n + 1 < nbunch else None
-            accs = passes(cur[0], cur[1])
+            accs = passes(n, cur[0], cur[1])
             if zg is not None:
-                cur = front_quantise(zg)
-            if n > 0:
-                finish(n - 1)
-            products(n, accs)
-        finish(nbunch - 1)
+                cur = front_quantise(n + 1, zg)
+            if len(tiles) == 2:
+                product(tiles[0], accs[0])
+                subtract(tiles[0], True)
+            for j in owed:
+                subtract(j, False)
+            product(tiles[-1], accs[-1])
+            owed = [tiles[-1]]
+        subtract(owed[0], False)

@@ -18,7 +18,7 @@ WIN = 448
 WSTEP = 192
 PAIR_G = ((0,), (0, 1), (0, 1), (1,))
 BUNCHES = (1, 2, 2, 2, 2, 2, 2, 2, 2, 2, 2, 2, 2, 2, 2, 2, 1)
-ZCHUNKS = (1, 2, 4, 8, 8, 9)
+ZCHUNKS = (1, 3, 4, 8, 8, 8)
 GROUPS = (4, 4, 4, 4, 4, 4, 4, 2, 1, 1)
 
 FLOPS = 2 * 2 * B * K * O
@@ -226,7 +226,9 @@ def tile_chebyshev_l3_sparsed32_stack_pa_t_kernel(tc, z, T1, T2, T0, mask, out_0
             x2s = outs[first][1]
             row = x2s[:, j - first, :]
             if on_gpsimd:
-                nc.gpsimd.tensor_tensor(out=row, in0=row, in1=t0b[:], op=ALU.subtract)
+                for h in range(2):
+                    cols = slice(h * (O // 2), (h + 1) * (O // 2))
+                    nc.gpsimd.tensor_tensor(out=row[:, cols], in0=row[:, cols], in1=t0b[:, cols], op=ALU.subtract)
             else:
                 nc.vector.tensor_tensor(out=row, in0=row, in1=t0ps[:], op=ALU.subtract)
             left[first] = left[first] - 1
@@ -237,22 +239,19 @@ def tile_chebyshev_l3_sparsed32_stack_pa_t_kernel(tc, z, T1, T2, T0, mask, out_0
         flip_pair(0)
         mask_pair(1)
         flip_pair(1)
-        quantise_pair(0)
         mask_pair(2)
         flip_pair(2)
-        quantise_pair(1)
+        quantise_pair(0)
         mask_pair(3)
         flip_pair(3)
-        quantise_pair(2)
+        quantise_pair(1)
         zg0 = front_flip(0)
+        quantise_pair(2)
         quantise_pair(3)
         cur = front_quantise(0, zg0)
 
         t0ps = ps_c.tile([P, O], F32, name="t0ps")
-        nc.tensor.matmul(out=t0ps[:], lhsT=ones[:], rhs=t0row[:], start=True, stop=True)
         t0b = const.tile([P, O], F32, name="t0b")
-        nc.scalar.copy(out=t0b[:], in_=t0ps[:])
-
         owed = []
         for n in range(nbunch):
             tiles = tiles_of[n]
@@ -260,11 +259,13 @@ def tile_chebyshev_l3_sparsed32_stack_pa_t_kernel(tc, z, T1, T2, T0, mask, out_0
             accs = passes(n, cur[0], cur[1])
             if zg is not None:
                 cur = front_quantise(n + 1, zg)
-            if len(tiles) == 2:
-                product(tiles[0], accs[0])
-                subtract(tiles[0], True)
-            for j in owed:
-                subtract(j, False)
-            product(tiles[-1], accs[-1])
-            owed = [tiles[-1]]
-        subtract(owed[0], False)
+            for jj in range(len(owed)):
+                subtract(owed[jj], jj == 1)
+            for jj in range(len(tiles)):
+                product(tiles[jj], accs[jj])
+            owed = tiles
+            if n == 0:
+                nc.tensor.matmul(out=t0ps[:], lhsT=ones[:], rhs=t0row[:], start=True, stop=True)
+                nc.scalar.copy(out=t0b[:], in_=t0ps[:])
+        for j in owed:
+            subtract(j, False)

from contextlib import ExitStack

import concourse.mybir as mybir
from concourse.masks import make_identity

F32 = mybir.dt.float32
BF16 = mybir.dt.bfloat16
U32 = mybir.dt.uint32
U8 = mybir.dt.uint8
FP8X4 = mybir.dt.float8_e4m3fn_x4
ALU = mybir.AluOpType

P = 128
B, K, O = 4096, 1024, 512
NT = B // P
STACKS, PAIRS, Q = 8, 4, 16
WIN = 448
WSTEP = 192
PAIR_G = ((0,), (0, 1), (0, 1), (1,))
BUNCHES = (1, 2, 2, 2, 2, 2, 2, 2, 2, 2, 2, 2, 2, 2, 2, 2, 1)
ZCHUNKS = (1, 3, 4, 8, 8, 8)
GROUPS = (4, 4, 4, 4, 4, 4, 4, 2, 1, 1)

FLOPS = 2 * 2 * B * K * O
BYTES = B * K * 2 + 3 * O * 352 * 2 + O * 2 + 2 * B * O * 4


def unit(w, g, i):
    if i == 0:
        return w
    if i == 3:
        return 10 + w
    return 2 + 4 * w + 2 * g + (i - 1)


def tile_chebyshev_l3_sparsed32_stack_pa_t_kernel(tc, z, T1, T2, T0, mask, out_0, out_1):
    nc = tc.nc
    with ExitStack() as ctx:
        const = ctx.enter_context(tc.tile_pool(name="const", bufs=1))
        wpool = ctx.enter_context(tc.tile_pool(name="wpool", bufs=1))
        zpool = ctx.enter_context(tc.tile_pool(name="zpool", bufs=1))
        gpool = ctx.enter_context(tc.tile_pool(name="gpool", bufs=3))
        opool = ctx.enter_context(tc.tile_pool(name="opool", bufs=5))
        ps_t = ctx.enter_context(tc.psum_pool(name="ps_t", bufs=2))
        ps_x = ctx.enter_context(tc.psum_pool(name="ps_x", bufs=2))
        ps_y = ctx.enter_context(tc.psum_pool(name="ps_y", bufs=3))
        ps_c = ctx.enter_context(tc.psum_pool(name="ps_c", bufs=1))
        ctx.enter_context(tc.manual_schedule())

        views = [a.rearrange("(s i q) k -> i q s k", s=STACKS, i=PAIRS, q=Q) for a in (mask, T1, T2)]
        raw = []
        for i in range(PAIRS):
            r = wpool.tile([P, 3, WIN], BF16, name="raw%d" % i)
            raw.append(r)
            for a in range(3):
                nc.sync.dma_start(out=r[:, a, :], in_=views[a][i, :, :, WSTEP * i : WSTEP * i + WIN])
        zv = z.rearrange("(p j) k -> p j k", j=NT)
        where = []
        for n, nj in enumerate(ZCHUNKS):
            j0 = len(where)
            zt_sb = zpool.tile([P, nj, K], BF16, name="z%d" % n)
            nc.sync.dma_start(out=zt_sb[:], in_=zv[:, j0 : j0 + nj, :])
            for s in range(nj):
                where.append((zt_sb, s))

        warm = const.tile([P, 8], F32, name="warm")
        warm2 = const.tile([P, 8], F32, name="warm2")
        nc.vector.memset(warm[:], 0.0)
        nc.scalar.copy(out=warm2[:], in_=warm[:])
        ident = const.tile([P, P], F32, name="ident")
        make_identity(nc, ident[:])
        t0row = const.tile([P, O], BF16, name="t0row")
        nc.vector.memset(t0row[:].bitcast(F32), 0.0)
        nc.scalar.dma_start(out=t0row[0:1, :], in_=T0.rearrange("(a n) -> a n", a=1))
        ones = const.tile([P, P], BF16, name="ones")
        nc.vector.memset(ones[:], 1.0)
        prod = []
        for i in range(PAIRS):
            pr = wpool.tile([P, 2, 512 * len(PAIR_G[i])], BF16, name="prod%d" % i)
            nc.vector.memset(pr[:].bitcast(F32), 0.0)
            prod.append(pr)

        wg = wpool.tile([P, 12, 512], BF16, name="wg", align_bytes=64)
        wgw = wg[:].bitcast(F32)
        wc = wpool.tile([P, 12 * P], U32, name="wc", align_bytes=64)
        ws = wpool.tile([P, 12 * P], U8, name="ws", align_bytes=64)

        def quantise_units(u0, nu):
            nc.vector.quantize_mx(
                out=wc[:, u0 * P : (u0 + nu) * P].bitcast(FP8X4),
                scales=ws[:, u0 * P : (u0 + nu) * P],
                in_=wg[:, u0 : u0 + nu, :].rearrange("p a b -> p (a b)"),
            )

        def mask_pair(i):
            off = WSTEP * i - 512 * PAIR_G[i][0]
            nc.vector.tensor_tensor(
                out=prod[i][:, :, off : off + WIN],
                in0=raw[i][:, 1:3, :],
                in1=raw[i][:, 0:1, :].to_broadcast([P, 2, WIN]),
                op=ALU.mult,
            )

        def flip_pair(i):
            kbase = 512 * PAIR_G[i][0]
            for g in PAIR_G[i]:
                if (i + g) % 2 == 0:
                    wt = ps_y.tile([P, 4, P], F32, name="wt", tag="y2")
                else:
                    wt = ps_x.tile([P, 4, P], F32, name="wt", tag="x1")
                for w in range(2):
                    words = prod[i][:, w, :].bitcast(F32)
                    for u in range(2):
                        c0 = (512 * g + 256 * u - kbase) // 2
                        nc.tensor.transpose(wt[:, 2 * w + u, :], words[:, c0 : c0 + P], ident[:])
                u0 = unit(0, g, i)
                du = unit(1, g, i) - u0
                nc.scalar.copy(
                    out=wgw[:, u0 : u0 + du + 1 : du, :].rearrange("p w (c u) -> p w c u", u=2),
                    in_=wt[:].rearrange("p (w u) c -> p w c u", u=2),
                )

        def quantise_pair(i):
            if i == 0 or i == 3:
                quantise_units(unit(0, PAIR_G[i][0], i), 2)
            else:
                for w in range(2):
                    for g in range(2):
                        quantise_units(unit(w, g, i), 1)

        tiles_of = []
        for size in BUNCHES:
            j0 = sum(len(t) for t in tiles_of)
            tiles_of.append(list(range(j0, j0 + size)))
        nbunch = len(tiles_of)

        def front_flip(n):
            tiles = tiles_of[n]
            zg = gpool.tile([P, len(tiles), K], BF16, name="zg", align_bytes=64)
            zgw = zg[:].bitcast(F32)
            zts = []
            for j in tiles:
                src, slot = where[j]
                words = src[:, slot, :].bitcast(F32)
                zt = ps_t.tile([P, 4, P], F32, name="zt")
                zts.append(zt)
                for c in range(4):
                    nc.tensor.transpose(zt[:, c, :], words[:, P * c : P * (c + 1)], ident[:])
            for jj in range(len(tiles)):
                nc.scalar.copy(
                    out=zgw[:, jj, :].rearrange("p (g b u) -> p g b u", g=2, b=P, u=2),
                    in_=zts[jj][:].rearrange("p (g u) b -> p g b u", g=2, u=2),
                )
            return zg

        def front_quantise(n, zg):
            width = len(tiles_of[n]) * 2 * P
            zc = gpool.tile([P, width], U32, name="zc", align_bytes=64)
            zs = gpool.tile([P, width], U8, name="zs", align_bytes=64)
            nc.vector.quantize_mx(
                out=zc[:].bitcast(FP8X4), scales=zs[:], in_=zg[:].rearrange("p j k -> p (j k)")
            )
            return zc, zs

        def passes(n, zc, zs):
            accs = []
            for jj in range(len(tiles_of[n])):
                x1 = ps_x.tile([P, O], F32, name="x1")
                y2 = ps_y.tile([P, O], F32, name="y2")
                accs.append((x1, y2))
                for w in range(2):
                    acc = accs[jj][w]
                    for c0, c1, g, u0, start, stop in (
                        (0, 128, 0, unit(w, 0, 0), True, True),
                        (128, 384, 0, unit(w, 0, 1), True, False),
                        (128, 384, 1, unit(w, 1, 1), False, True),
                        (384, 512, 1, unit(w, 1, 3), True, True),
                    ):
                        l0 = (2 * jj + g) * P
                        r0 = u0 * P
                        nc.tensor.matmul_mx(
                            out=acc[:, c0:c1],
                            lhsT=zc[:, l0 : l0 + P].bitcast(FP8X4),
                            lhsT_scale=zs[:, l0 : l0 + P],
                            rhs=wc[:, r0 : r0 + c1 - c0].bitcast(FP8X4),
                            rhs_scale=ws[:, r0 : r0 + c1 - c0],
                            start=start,
                            stop=stop,
                        )
            return accs

        o0v = out_0.rearrange("(p j) o -> p j o", j=NT)
        o1v = out_1.rearrange("(p j) o -> p j o", j=NT)
        span = []
        for size in GROUPS:
            first = len(span)
            for k in range(size):
                span.append((first, size))
        outs = {}
        left = {}

        def product(j, acc):
            first, size = span[j]
            if j == first:
                x1new = opool.tile([P, size, O], F32, name="x1s")
                x2new = opool.tile([P, size, O], F32, name="x2s")
                outs[first] = (x1new, x2new)
                left[first] = size
            x1s, x2s = outs[first]
            nat1 = x1s[:, j - first, :].rearrange("p (s r) -> p s r", s=STACKS)
            nat2 = x2s[:, j - first, :].rearrange("p (s r) -> p s r", s=STACKS)
            nc.scalar.copy(out=nat1, in_=acc[0][:].rearrange("p (r s) -> p s r", s=STACKS))
            nc.vector.scalar_tensor_tensor(
                out=nat2,
                in0=acc[1][:].rearrange("p (r s) -> p s r", s=STACKS),
                scalar=2.0,
                in1=nat1,
                op0=ALU.mult,
                op1=ALU.mult,
            )
            if j == first + size - 1:
                nc.sync.dma_start(out=o0v[:, first : first + size, :], in_=x1s[:])

        def subtract(j, on_gpsimd):
            first, size = span[j]
            x2s = outs[first][1]
            row = x2s[:, j - first, :]
            if on_gpsimd:
                for h in range(2):
                    cols = slice(h * (O // 2), (h + 1) * (O // 2))
                    nc.gpsimd.tensor_tensor(out=row[:, cols], in0=row[:, cols], in1=t0b[:, cols], op=ALU.subtract)
            else:
                nc.vector.tensor_tensor(out=row, in0=row, in1=t0ps[:], op=ALU.subtract)
            left[first] = left[first] - 1
            if left[first] == 0:
                nc.sync.dma_start(out=o1v[:, first : first + size, :], in_=x2s[:])

        mask_pair(0)
        flip_pair(0)
        mask_pair(1)
        flip_pair(1)
        mask_pair(2)
        flip_pair(2)
        quantise_pair(0)
        mask_pair(3)
        flip_pair(3)
        quantise_pair(1)
        zg0 = front_flip(0)
        quantise_pair(2)
        quantise_pair(3)
        cur = front_quantise(0, zg0)

        t0ps = ps_c.tile([P, O], F32, name="t0ps")
        t0b = const.tile([P, O], F32, name="t0b")
        owed = []
        for n in range(nbunch):
            tiles = tiles_of[n]
            zg = front_flip(n + 1) if n + 1 < nbunch else None
            accs = passes(n, cur[0], cur[1])
            if zg is not None:
                cur = front_quantise(n + 1, zg)
            for jj in range(len(owed)):
                subtract(owed[jj], jj == 1)
            for jj in range(len(tiles)):
                product(tiles[jj], accs[jj])
            owed = tiles
            if n == 0:
                nc.tensor.matmul(out=t0ps[:], lhsT=ones[:], rhs=t0row[:], start=True, stop=True)
                nc.scalar.copy(out=t0b[:], in_=t0ps[:])
        for j in owed:
            subtract(j, False)
